import numpy as np
import ml_dtypes


def mxq(x, axis, fmt="e4m3"):
    dtype, down = {"e4m3": (ml_dtypes.float8_e4m3fn, 7), "e5m2": (ml_dtypes.float8_e5m2, 14)}[fmt]
    v = np.moveaxis(np.asarray(x, np.float32).astype(ml_dtypes.bfloat16).astype(np.float64), axis, -1)
    blocks = v.reshape(v.shape[:-1] + (-1, 32))
    amax = np.abs(blocks).max(-1, keepdims=True)
    byte = np.maximum(np.where(amax > 0, np.frexp(amax)[1] - 1 + 127, 0) - down, 1)
    scale = np.exp2(byte - 127.0)
    codes = (blocks / scale).astype(np.float32).astype(dtype).astype(np.float64)
    return np.moveaxis((codes * scale).reshape(v.shape), -1, axis)


WIDE = False


def mx_kscale(k):
    if not WIDE:
        return np.ones(k)
    levels = np.array([10, -10, 5, -5, 0])
    a = np.random.permutation(np.resize(levels, k // 512 * 4)).reshape(k // 512, 4)
    idx = np.arange(k)
    return np.exp2(a[idx // 512, idx % 128 // 32])


BF16 = ml_dtypes.bfloat16


def bf(x):
    return np.asarray(x, np.float32).astype(BF16)


def f64(x):
    return np.asarray(x).astype(np.float64)


E2M1 = np.array([0.0, 0.5, 1.0, 1.5, 2.0, 3.0, 4.0, 6.0, -0.0, -0.5, -1.0, -1.5, -2.0, -3.0, -4.0, -6.0])


def pack_weight(w, fmt):
    k, n = w.shape
    w = f64(bf(w)).reshape(k // 32, 32, n)
    amax = np.abs(w).max(1)
    if fmt == "e4m3":
        byte = np.frexp(amax)[1] - 1 + 127 - 7
    else:
        mant, ex = np.frexp(amax / 6.0)
        byte = np.where(mant > 0.5, ex, ex - 1) + 127
    byte = np.clip(np.where(amax > 0, byte, 1), 1, 254)
    scaled = (w * np.exp2(127.0 - byte)[:, None, :]).reshape(k, n).astype(np.float32)
    by_word = np.ascontiguousarray(scaled.reshape(k // 512, 128, 4, n).transpose(0, 1, 3, 2))
    if fmt == "e4m3":
        words = by_word.astype(ml_dtypes.float8_e4m3fn).view(np.uint8)
    else:
        c = by_word.astype(ml_dtypes.float4_e2m1fn).view(np.uint8) & 0xF
        words = c[..., 0::2] | (c[..., 1::2] << 4)
    return np.ascontiguousarray(words), np.ascontiguousarray(byte.astype(np.uint8).reshape(k // 512, 16, n))


def unpack_weight(words, scales, fmt):
    g, p, n, _ = words.shape
    if fmt == "e4m3":
        vals = np.ascontiguousarray(words).view(ml_dtypes.float8_e4m3fn).astype(np.float64)
    else:
        nib = np.empty((g, p, n, 4), np.uint8)
        nib[..., 0::2] = words & 0xF
        nib[..., 1::2] = words >> 4
        vals = E2M1[nib]
    vals = vals * np.repeat(np.exp2(scales.astype(np.float64) - 127.0), 8, axis=1)[..., None]
    return vals.transpose(0, 1, 3, 2).reshape(g * 512, n)


BS, D, R = 128, 4096, 4096
ALPHA = 1.0


def setup_inputs():
    s = mx_kscale(D)
    f = np.random.standard_normal((BS, D)) + np.random.standard_normal((BS, 1)) * np.random.standard_normal((1, D))
    features = bf(f * s)
    words, scales = pack_weight(np.random.standard_normal((D, R)) * np.sqrt(0.5 / (D * R)) / s[:, None], "e4m3")
    return {"features": features, "P_words": words, "P_scales": scales}


def reference(features, P_words, P_scales):
    Z = mxq(f64(features), 1, "e4m3") @ unpack_weight(P_words, P_scales, "e4m3")
    sq_norm = np.sum(Z * Z, axis=1)
    Zq = mxq(Z, 1, "e4m3")
    sq = sq_norm[:, None] + sq_norm[None, :] - 2.0 * (Zq @ Zq.T)
    sq = np.maximum(sq, 0.0)
    eye = np.eye(Z.shape[0], dtype=bool)
    dist = np.where(eye, 0.0, np.sqrt(np.where(eye, 1.0, sq)))
    adjacency_pre = np.exp(-ALPHA * dist)
    d_inv_sqrt = 1.0 / np.sqrt(np.sum(adjacency_pre, axis=1))
    normalized = d_inv_sqrt[:, None] * adjacency_pre * d_inv_sqrt[None, :]
    return (normalized, adjacency_pre)

@@ -1,0 +1,293 @@
+from contextlib import ExitStack
+
+import concourse.mybir as mybir
+from concourse.masks import make_identity
+
+F32 = mybir.dt.float32
+BF16 = mybir.dt.bfloat16
+I32 = mybir.dt.int32
+U32 = mybir.dt.uint32
+U8 = mybir.dt.uint8
+FP8X4 = mybir.dt.float8_e4m3fn_x4
+ACT = mybir.ActivationFunctionType
+ALU = mybir.AluOpType
+AX = mybir.AxisListType
+
+P = 128
+D = 4096
+R = 4096
+KG = 8
+NB = 512
+FLOPS = 2 * P * D * R + 2 * P * P * R
+
+PIN = True
+SCALES_ON_GPSIMD = False
+
+GROUPS = (
+    (0, 2048, (1, 1, 1, 1, 1, 1, 1, 1)),
+    (2048, 1024, (2, 2, 2, 2)),
+    (3072, 512, (4, 4)),
+    (3584, 512, (4, 2, 1, 1)),
+)
+
+
+def tile_metric_learning_based_adjacency_matrix_w_kernel(
+    tc, features, P_words, P_scales, out_0, out_1
+):
+    nc = tc.nc
+    with ExitStack() as ctx:
+        if PIN:
+            ctx.enter_context(tc.manual_schedule())
+        const = ctx.enter_context(tc.tile_pool(name="const", bufs=1))
+        wpool = ctx.enter_context(tc.tile_pool(name="weights", bufs=1))
+        work = ctx.enter_context(tc.tile_pool(name="work", bufs=3))
+        zps = ctx.enter_context(tc.psum_pool(name="zps", bufs=6))
+        tps = ctx.enter_context(tc.psum_pool(name="tps", bufs=1))
+        gps = ctx.enter_context(tc.psum_pool(name="gps", bufs=1))
+
+        planes = [
+            const.tile([P, R], U8, align_bytes=64, name="plane%d" % h) for h in range(2)
+        ]
+        for h in range(2):
+            nc.vector.memset(planes[h][:].bitcast(I32), 0)
+        one = const.tile([P, 1], F32, name="one")
+        nc.vector.memset(one[:], 1.0)
+        mhalf = const.tile([P, 1], F32, name="mhalf")
+        nc.vector.memset(mhalf[:], -0.5)
+        warm = const.tile([P, 1], F32, name="warm")
+        nc.scalar.activation(out=warm[:], in_=one[:], func=ACT.Sqrt)
+        ident = const.tile([P, P], F32, name="ident")
+        make_identity(nc, ident[:])
+        identb = const.tile([P, P], BF16, name="identb")
+        nc.vector.tensor_copy(out=identb[:], in_=ident[:])
+        negdiag = const.tile([P, P], F32, name="negdiag")
+        nc.vector.tensor_single_scalar(out=negdiag[:], in_=ident[:], scalar=-3.0e38, op=ALU.mult)
+
+        x_sb = [const.tile([P, D // 2], BF16, name="x%d" % h) for h in range(2)]
+        for h in range(2):
+            nc.sync.dma_start(out=x_sb[h][:], in_=features[:, h * (D // 2) : (h + 1) * (D // 2)])
+        for h in range(2):
+            for q in range(4):
+                if SCALES_ON_GPSIMD:
+                    nc.gpsimd.dma_start(
+                        out=planes[h][32 * q : 32 * q + 16, :].bitcast(F32),
+                        in_=P_scales[4 * h : 4 * h + 4, 4 * q : 4 * q + 4, :].bitcast(F32),
+                    )
+                else:
+                    nc.sync.dma_start(
+                        out=planes[h][32 * q : 32 * q + 16, :].bitcast(I32),
+                        in_=P_scales[4 * h : 4 * h + 4, 4 * q : 4 * q + 4, :].bitcast(I32),
+                    )
+        words = P_words.rearrange("g p n t -> g p (n t)").bitcast(I32)
+        wt = {}
+        for gi, (c0, ncols, cuts) in enumerate(GROUPS):
+            g0 = 0
+            for ng in cuts:
+                t = wpool.tile([P, ng, ncols], U32, align_bytes=64, name="w%d_%d" % (gi, g0))
+                nc.sync.dma_start(
+                    out=t[:].bitcast(I32),
+                    in_=words[g0 : g0 + ng, :, c0 : c0 + ncols].rearrange("g p n -> p g n"),
+                )
+                for j in range(ng):
+                    wt[(gi, g0 + j)] = (t, j)
+                g0 += ng
+
+        fq = []
+        fs = []
+        gf = []
+        ft = []
+        for j in range(4):
+            xw = x_sb[j // 2][:].bitcast(F32)
+            tp = zps.tile([P, NB], F32, tag="z", name="ft%d" % j)
+            for gl in range(2):
+                base = 256 * ((2 * j + gl) % 4)
+                for u in range(2):
+                    nc.tensor.transpose(
+                        tp[:, (2 * gl + u) * P : (2 * gl + u + 1) * P],
+                        xw[:, base + u : base + 256 : 2],
+                        ident[:],
+                    )
+            ft.append(tp)
+        for j in range(4):
+            g_t = const.tile([P, 1024], BF16, align_bytes=64, name="gf%d" % j)
+            dst = g_t[:].bitcast(F32).rearrange("p (g i u) -> p g i u", g=2, u=2)
+            src = ft[j][:].rearrange("p (g u i) -> p g i u", g=2, u=2)
+            if j % 2 == 0:
+                nc.vector.tensor_copy(out=dst, in_=src)
+            else:
+                nc.scalar.copy(out=dst, in_=src)
+            gf.append(g_t)
+        for j in range(4):
+            c_t = const.tile([P, 256], U32, align_bytes=64, name="fq%d" % j)
+            s_t = const.tile([P, 256], U8, align_bytes=64, name="fs%d" % j)
+            nc.vector.quantize_mx(out=c_t[:].bitcast(FP8X4), scales=s_t[:], in_=gf[j][:])
+            fq.append(c_t)
+            fs.append(s_t)
+
+        ncol = const.tile([P, 8], F32, name="ncol")
+        gram = gps.tile([P, P], F32, name="gram")
+        zt = {}
+        zb = {}
+        tt = {}
+        gz = {}
+        zq = {}
+
+        def passes(gi, g):
+            c0, ncols, cuts = GROUPS[gi]
+            t, j = wt[(gi, g)]
+            k = 4 * (g % 4)
+            pl = planes[g // 4]
+            for b in range(ncols // NB):
+                c = c0 // NB + b
+                if g == 0:
+                    zt[c] = zps.tile([P, NB], F32, tag="z", name="z%d" % c)
+                nc.tensor.matmul_mx(
+                    out=zt[c][:],
+                    lhsT=fq[g // 2][:, (g % 2) * P : (g % 2 + 1) * P].bitcast(FP8X4),
+                    lhsT_scale=fs[g // 2][:, (g % 2) * P : (g % 2 + 1) * P],
+                    rhs=t[:, j, b * NB : (b + 1) * NB].bitcast(FP8X4),
+                    rhs_scale=pl[k:P, c * NB : (c + 1) * NB],
+                    start=(g == 0),
+                    stop=(g == KG - 1),
+                )
+
+        def s2a(c):
+            zb[c] = work.tile([P, NB], BF16, tag="zb", bufs=4, name="zb%d" % c)
+            nc.vector.tensor_copy(out=zb[c][:], in_=zt[c][:])
+            junk = work.tile([P, NB], BF16, tag="junk", bufs=2, name="junk%d" % c)
+            nc.scalar.activation(
+                out=junk[:], in_=zt[c][:], func=ACT.Square, accum_out=ncol[:, c : c + 1]
+            )
+
+        def s2b(c):
+            tt[c] = tps.tile([P, NB], BF16, tag="t", name="tt%d" % c)
+            for t in range(4):
+                nc.tensor.transpose(
+                    tt[c][:, t * P : (t + 1) * P], zb[c][:, t * P : (t + 1) * P], identb[:]
+                )
+
+        def s2c(c, eng):
+            gz[c] = work.tile([P, NB], BF16, tag="gz", align_bytes=64, name="gz%d" % c)
+            dst = gz[c][:].rearrange("p (i t) -> p i t", t=4)
+            src = tt[c][:].rearrange("p (t i) -> p i t", t=4)
+            if eng == "v":
+                nc.vector.tensor_copy(out=dst, in_=src)
+            else:
+                nc.scalar.copy(out=dst, in_=src)
+
+        def s2d(c):
+            w_t = work.tile([P, P], U32, tag="zq", align_bytes=64, name="zq%d" % c)
+            s_t = work.tile([P, P], U8, tag="zs", align_bytes=64, name="zs%d" % c)
+            nc.vector.quantize_mx(out=w_t[:].bitcast(FP8X4), scales=s_t[:], in_=gz[c][:])
+            zq[c] = (w_t, s_t)
+
+        def s2e(c):
+            w_t, s_t = zq[c]
+            nc.tensor.matmul_mx(
+                out=gram[:],
+                lhsT=w_t[:].bitcast(FP8X4),
+                lhsT_scale=s_t[:],
+                rhs=w_t[:].bitcast(FP8X4),
+                rhs_scale=s_t[:],
+                start=(c == 0),
+                stop=(c == 7),
+            )
+
+        for g in range(KG):
+            passes(0, g)
+        s2a(0)
+        s2b(0)
+        s2a(1)
+        s2c(0, "s")
+        passes(1, 0)
+        passes(1, 1)
+        s2b(1)
+        s2a(2)
+        s2d(0)
+        s2c(1, "s")
+        s2e(0)
+        passes(1, 2)
+        passes(1, 3)
+        s2b(2)
+        s2a(3)
+        s2d(1)
+        s2c(2, "s")
+        s2e(1)
+        passes(1, 4)
+        passes(1, 5)
+        s2b(3)
+        s2d(2)
+        s2c(3, "s")
+        s2e(2)
+        passes(1, 6)
+        passes(1, 7)
+        s2d(3)
+        s2e(3)
+        s2a(4)
+        s2b(4)
+        s2a(5)
+        s2c(4, "s")
+        for g in range(4):
+            passes(2, g)
+        s2b(5)
+        s2d(4)
+        s2c(5, "s")
+        s2e(4)
+        for g in range(4, 8):
+            passes(2, g)
+        s2d(5)
+        s2e(5)
+        s2a(6)
+        s2b(6)
+        for g in range(4):
+            passes(3, g)
+        s2c(6, "s")
+        s2d(6)
+        passes(3, 4)
+        passes(3, 5)
+        s2e(6)
+        passes(3, 6)
+        passes(3, 7)
+
+        s2a(7)
+        s2b(7)
+        nsum = const.tile([P, 1], F32, name="nsum")
+        nc.vector.tensor_reduce(out=nsum[:], in_=ncol[:], axis=AX.X, op=ALU.add)
+        njp = zps.tile([P, NB], F32, tag="z", name="njp")
+        nc.tensor.matmul(
+            out=njp[:, 0:P], lhsT=nsum[:, 0:1].to_broadcast([P, P]), rhs=ident[:], start=True, stop=True
+        )
+        s2c(7, "v")
+        s2d(7)
+        hsum = const.tile([P, P], F32, name="hsum")
+        nc.vector.scalar_tensor_tensor(
+            out=hsum[:], in0=njp[:, 0:P], scalar=nsum[:, 0:1], in1=negdiag[:], op0=ALU.add, op1=ALU.add
+        )
+        s2e(7)
+        sq = const.tile([P, P], F32, name="sq")
+        nc.vector.scalar_tensor_tensor(
+            out=sq[:], in0=gram[:], scalar=-2.0, in1=hsum[:], op0=ALU.mult, op1=ALU.add
+        )
+        sqc = const.tile([P, P], F32, name="sqc")
+        nc.vector.tensor_scalar(
+            out=sqc[:], in0=sq[:], scalar1=1.0e-30, scalar2=1.0e35, op0=ALU.max, op1=ALU.min
+        )
+        dist = const.tile([P, P], F32, name="dist")
+        nc.scalar.activation(out=dist[:], in_=sqc[:], func=ACT.Sqrt)
+        araw = const.tile([P, P], F32, name="araw")
+        deg = const.tile([P, 1], F32, name="deg")
+        nc.scalar.activation(out=araw[:], in_=dist[:], func=ACT.Exp, scale=-1.0, accum_out=deg[:])
+        dinv = const.tile([P, 1], F32, name="dinv")
+        nc.gpsimd.tensor_tensor(out=dinv[:], in0=deg[:], in1=mhalf[:], op=ALU.pow)
+        adj = const.tile([P, P], F32, name="adj")
+        nc.vector.tensor_tensor(out=adj[:], in0=araw[:], in1=ident[:], op=ALU.max)
+        nc.sync.dma_start(out=out_1[:, :], in_=adj[:])
+        djp = zps.tile([P, NB], F32, tag="z", name="djp")
+        nc.tensor.matmul(
+            out=djp[:, 0:P], lhsT=dinv[:, 0:1].to_broadcast([P, P]), rhs=ident[:], start=True, stop=True
+        )
+        norm = const.tile([P, P], F32, name="norm")
+        nc.vector.scalar_tensor_tensor(
+            out=norm[:], in0=adj[:], scalar=dinv[:, 0:1], in1=djp[:, 0:P], op0=ALU.mult, op1=ALU.mult
+        )
+        nc.sync.dma_start(out=out_0[:, :], in_=norm[:])

@@ -21,7 +21,7 @@ NB = 512
 FLOPS = 2 * P * D * R + 2 * P * P * R
 
 PIN = True
-SCALES_ON_GPSIMD = False
+SCALES_ON_GPSIMD = True
 
 GROUPS = (
     (0, 2048, (1, 1, 1, 1, 1, 1, 1, 1)),

@@ -21,7 +21,6 @@ NB = 512
 FLOPS = 2 * P * D * R + 2 * P * P * R
 
 PIN = True
-SCALES_ON_GPSIMD = True
 
 GROUPS = (
     (0, 2048, (1, 1, 1, 1, 1, 1, 1, 1)),
@@ -45,11 +44,8 @@ def tile_metric_learning_based_adjacency_matrix_w_kernel(
         tps = ctx.enter_context(tc.psum_pool(name="tps", bufs=1))
         gps = ctx.enter_context(tc.psum_pool(name="gps", bufs=1))
 
-        planes = [
-            const.tile([P, R], U8, align_bytes=64, name="plane%d" % h) for h in range(2)
-        ]
-        for h in range(2):
-            nc.vector.memset(planes[h][:].bitcast(I32), 0)
+        planes = const.tile([P, 2, R], U8, align_bytes=64, name="planes")
+        nc.vector.memset(planes[:].bitcast(I32), 0)
         one = const.tile([P, 1], F32, name="one")
         nc.vector.memset(one[:], 1.0)
         mhalf = const.tile([P, 1], F32, name="mhalf")
@@ -67,17 +63,18 @@ def tile_metric_learning_based_adjacency_matrix_w_kernel(
         for h in range(2):
             nc.sync.dma_start(out=x_sb[h][:], in_=features[:, h * (D // 2) : (h + 1) * (D // 2)])
         for h in range(2):
-            for q in range(4):
-                if SCALES_ON_GPSIMD:
-                    nc.gpsimd.dma_start(
-                        out=planes[h][32 * q : 32 * q + 16, :].bitcast(F32),
-                        in_=P_scales[4 * h : 4 * h + 4, 4 * q : 4 * q + 4, :].bitcast(F32),
-                    )
-                else:
-                    nc.sync.dma_start(
-                        out=planes[h][32 * q : 32 * q + 16, :].bitcast(I32),
-                        in_=P_scales[4 * h : 4 * h + 4, 4 * q : 4 * q + 4, :].bitcast(I32),
-                    )
+            for q in range(2):
+                nc.sync.dma_start(
+                    out=planes[32 * q : 32 * q + 16, h, :].bitcast(I32),
+                    in_=P_scales[4 * h : 4 * h + 4, 4 * q : 4 * q + 4, :].bitcast(I32),
+                )
+        by_row = P_scales.rearrange("(h s) q n -> q s h n", h=2)
+        for q in range(2, 4):
+            for r in range(4):
+                nc.gpsimd.dma_start(
+                    out=planes[32 * q + r : 32 * q + r + 16 : 4, :, :].bitcast(F32),
+                    in_=by_row[4 * q + r].bitcast(F32),
+                )
         words = P_words.rearrange("g p n t -> g p (n t)").bitcast(I32)
         wt = {}
         for gi, (c0, ncols, cuts) in enumerate(GROUPS):
@@ -136,7 +133,7 @@ def tile_metric_learning_based_adjacency_matrix_w_kernel(
             c0, ncols, cuts = GROUPS[gi]
             t, j = wt[(gi, g)]
             k = 4 * (g % 4)
-            pl = planes[g // 4]
+            h = g // 4
             for b in range(ncols // NB):
                 c = c0 // NB + b
                 if g == 0:
@@ -146,7 +143,7 @@ def tile_metric_learning_based_adjacency_matrix_w_kernel(
                     lhsT=fq[g // 2][:, (g % 2) * P : (g % 2 + 1) * P].bitcast(FP8X4),
                     lhsT_scale=fs[g // 2][:, (g % 2) * P : (g % 2 + 1) * P],
                     rhs=t[:, j, b * NB : (b + 1) * NB].bitcast(FP8X4),
-                    rhs_scale=pl[k:P, c * NB : (c + 1) * NB],
+                    rhs_scale=planes[k:P, h, c * NB : (c + 1) * NB],
                     start=(g == 0),
                     stop=(g == KG - 1),
                 )

@@ -23,10 +23,10 @@ FLOPS = 2 * P * D * R + 2 * P * P * R
 PIN = True
 
 GROUPS = (
-    (0, 2048, (1, 1, 1, 1, 1, 1, 1, 1)),
-    (2048, 1024, (2, 2, 2, 2)),
-    (3072, 512, (4, 4)),
-    (3584, 512, (4, 2, 1, 1)),
+    (0, 2048, 512, (1, 1, 1, 1, 1, 1, 1, 1)),
+    (2048, 1024, 512, (2, 2, 2, 2)),
+    (3072, 512, 512, (4, 2, 1, 1)),
+    (3584, 512, 256, (4, 2, 1, 1)),
 )
 
 
@@ -77,7 +77,7 @@ def tile_metric_learning_based_adjacency_matrix_w_kernel(
                 )
         words = P_words.rearrange("g p n t -> g p (n t)").bitcast(I32)
         wt = {}
-        for gi, (c0, ncols, cuts) in enumerate(GROUPS):
+        for gi, (c0, ncols, width, cuts) in enumerate(GROUPS):
             g0 = 0
             for ng in cuts:
                 t = wpool.tile([P, ng, ncols], U32, align_bytes=64, name="w%d_%d" % (gi, g0))
@@ -121,7 +121,7 @@ def tile_metric_learning_based_adjacency_matrix_w_kernel(
             fq.append(c_t)
             fs.append(s_t)
 
-        ncol = const.tile([P, 8], F32, name="ncol")
+        ncol = const.tile([P, 9], F32, name="ncol")
         gram = gps.tile([P, P], F32, name="gram")
         zt = {}
         zb = {}
@@ -130,30 +130,30 @@ def tile_metric_learning_based_adjacency_matrix_w_kernel(
         zq = {}
 
         def passes(gi, g):
-            c0, ncols, cuts = GROUPS[gi]
+            c0, ncols, width, cuts = GROUPS[gi]
             t, j = wt[(gi, g)]
             k = 4 * (g % 4)
             h = g // 4
-            for b in range(ncols // NB):
-                c = c0 // NB + b
+            for b in range(ncols // width):
+                col = c0 + b * width
                 if g == 0:
-                    zt[c] = zps.tile([P, NB], F32, tag="z", name="z%d" % c)
+                    zt[col] = zps.tile([P, NB], F32, tag="z", name="z%d" % col)
                 nc.tensor.matmul_mx(
-                    out=zt[c][:],
+                    out=zt[col][:, 0:width],
                     lhsT=fq[g // 2][:, (g % 2) * P : (g % 2 + 1) * P].bitcast(FP8X4),
                     lhsT_scale=fs[g // 2][:, (g % 2) * P : (g % 2 + 1) * P],
-                    rhs=t[:, j, b * NB : (b + 1) * NB].bitcast(FP8X4),
-                    rhs_scale=planes[k:P, h, c * NB : (c + 1) * NB],
+                    rhs=t[:, j, b * width : (b + 1) * width].bitcast(FP8X4),
+                    rhs_scale=planes[k:P, h, col : col + width],
                     start=(g == 0),
                     stop=(g == KG - 1),
                 )
 
         def s2a(c):
             zb[c] = work.tile([P, NB], BF16, tag="zb", bufs=4, name="zb%d" % c)
-            nc.vector.tensor_copy(out=zb[c][:], in_=zt[c][:])
+            nc.vector.tensor_copy(out=zb[c][:], in_=zt[c * NB][:])
             junk = work.tile([P, NB], BF16, tag="junk", bufs=2, name="junk%d" % c)
             nc.scalar.activation(
-                out=junk[:], in_=zt[c][:], func=ACT.Square, accum_out=ncol[:, c : c + 1]
+                out=junk[:], in_=zt[c * NB][:], func=ACT.Square, accum_out=ncol[:, c : c + 1]
             )
 
         def s2b(c):
@@ -230,31 +230,42 @@ def tile_metric_learning_based_adjacency_matrix_w_kernel(
         s2d(4)
         s2c(5, "s")
         s2e(4)
-        for g in range(4, 8):
-            passes(2, g)
+        passes(2, 4)
+        passes(2, 5)
         s2d(5)
         s2e(5)
+        passes(2, 6)
+        passes(2, 7)
         s2a(6)
         s2b(6)
         for g in range(4):
             passes(3, g)
         s2c(6, "s")
         s2d(6)
-        passes(3, 4)
-        passes(3, 5)
         s2e(6)
-        passes(3, 6)
-        passes(3, 7)
+        for g in range(4, 8):
+            passes(3, g)
 
-        s2a(7)
+        half = NB // 2
+        z7a = zt[7 * NB]
+        z7b = zt[7 * NB + half]
+        zb[7] = work.tile([P, NB], BF16, tag="zb", bufs=4, name="zb7")
+        junk_b = work.tile([P, NB], BF16, tag="junk", bufs=2, name="junk7b")
+        junk_a = work.tile([P, NB], BF16, tag="junk", bufs=2, name="junk7a")
+        nc.vector.tensor_copy(out=zb[7][:, 0:half], in_=z7a[:, 0:half])
+        nc.scalar.activation(
+            out=junk_b[:, 0:half], in_=z7b[:, 0:half], func=ACT.Square, accum_out=ncol[:, 8:9]
+        )
+        nc.vector.tensor_copy(out=zb[7][:, half:NB], in_=z7b[:, 0:half])
+        nc.scalar.activation(
+            out=junk_a[:, 0:half], in_=z7a[:, 0:half], func=ACT.Square, accum_out=ncol[:, 7:8]
+        )
         s2b(7)
         nsum = const.tile([P, 1], F32, name="nsum")
         nc.vector.tensor_reduce(out=nsum[:], in_=ncol[:], axis=AX.X, op=ALU.add)
         njp = zps.tile([P, NB], F32, tag="z", name="njp")
-        nc.tensor.matmul(
-            out=njp[:, 0:P], lhsT=nsum[:, 0:1].to_broadcast([P, P]), rhs=ident[:], start=True, stop=True
-        )
-        s2c(7, "v")
+        nc.tensor.transpose(njp[:, 0:P], nsum[:, 0:1].to_broadcast([P, P]), ident[:])
+        s2c(7, "s")
         s2d(7)
         hsum = const.tile([P, P], F32, name="hsum")
         nc.vector.scalar_tensor_tensor(
@@ -280,9 +291,7 @@ def tile_metric_learning_based_adjacency_matrix_w_kernel(
         nc.vector.tensor_tensor(out=adj[:], in0=araw[:], in1=ident[:], op=ALU.max)
         nc.sync.dma_start(out=out_1[:, :], in_=adj[:])
         djp = zps.tile([P, NB], F32, tag="z", name="djp")
-        nc.tensor.matmul(
-            out=djp[:, 0:P], lhsT=dinv[:, 0:1].to_broadcast([P, P]), rhs=ident[:], start=True, stop=True
-        )
+        nc.tensor.transpose(djp[:, 0:P], dinv[:, 0:1].to_broadcast([P, P]), ident[:])
         norm = const.tile([P, P], F32, name="norm")
         nc.vector.scalar_tensor_tensor(
             out=norm[:], in0=adj[:], scalar=dinv[:, 0:1], in1=djp[:, 0:P], op0=ALU.mult, op1=ALU.mult

@@ -23,9 +23,8 @@ FLOPS = 2 * P * D * R + 2 * P * P * R
 PIN = True
 
 GROUPS = (
-    (0, 2048, 512, (1, 1, 1, 1, 1, 1, 1, 1)),
-    (2048, 1024, 512, (2, 2, 2, 2)),
-    (3072, 512, 512, (4, 2, 1, 1)),
+    (0, 2560, 512, (1, 1, 1, 1, 1, 1, 1, 1)),
+    (2560, 1024, 512, (2, 2, 2, 1, 1)),
     (3584, 512, 256, (4, 2, 1, 1)),
 )
 
@@ -63,13 +62,13 @@ def tile_metric_learning_based_adjacency_matrix_w_kernel(
         for h in range(2):
             nc.sync.dma_start(out=x_sb[h][:], in_=features[:, h * (D // 2) : (h + 1) * (D // 2)])
         for h in range(2):
-            for q in range(2):
+            for q in range(1):
                 nc.sync.dma_start(
                     out=planes[32 * q : 32 * q + 16, h, :].bitcast(I32),
                     in_=P_scales[4 * h : 4 * h + 4, 4 * q : 4 * q + 4, :].bitcast(I32),
                 )
         by_row = P_scales.rearrange("(h s) q n -> q s h n", h=2)
-        for q in range(2, 4):
+        for q in range(1, 4):
             for r in range(4):
                 nc.gpsimd.dma_start(
                     out=planes[32 * q + r : 32 * q + r + 16 : 4, :, :].bitcast(F32),
@@ -148,9 +147,11 @@ def tile_metric_learning_based_adjacency_matrix_w_kernel(
                     stop=(g == KG - 1),
                 )
 
-        def s2a(c):
+        def s2av(c):
             zb[c] = work.tile([P, NB], BF16, tag="zb", bufs=4, name="zb%d" % c)
             nc.vector.tensor_copy(out=zb[c][:], in_=zt[c * NB][:])
+
+        def s2as(c):
             junk = work.tile([P, NB], BF16, tag="junk", bufs=2, name="junk%d" % c)
             nc.scalar.activation(
                 out=junk[:], in_=zt[c * NB][:], func=ACT.Square, accum_out=ncol[:, c : c + 1]
@@ -192,59 +193,48 @@ def tile_metric_learning_based_adjacency_matrix_w_kernel(
 
         for g in range(KG):
             passes(0, g)
-        s2a(0)
+        s2av(0)
+        s2as(0)
         s2b(0)
-        s2a(1)
+        s2av(1)
         s2c(0, "s")
+        s2as(1)
         passes(1, 0)
         passes(1, 1)
-        s2b(1)
-        s2a(2)
-        s2d(0)
-        s2c(1, "s")
-        s2e(0)
-        passes(1, 2)
-        passes(1, 3)
-        s2b(2)
-        s2a(3)
-        s2d(1)
-        s2c(2, "s")
-        s2e(1)
-        passes(1, 4)
-        passes(1, 5)
-        s2b(3)
-        s2d(2)
-        s2c(3, "s")
-        s2e(2)
-        passes(1, 6)
-        passes(1, 7)
-        s2d(3)
-        s2e(3)
-        s2a(4)
-        s2b(4)
-        s2a(5)
-        s2c(4, "s")
+        for c in range(1, 5):
+            s2b(c)
+            if c < 4:
+                s2av(c + 1)
+            s2d(c - 1)
+            s2c(c, "s")
+            if c < 4:
+                s2as(c + 1)
+            s2e(c - 1)
+            if c < 3:
+                passes(1, 2 * c)
+                passes(1, 2 * c + 1)
+            else:
+                passes(1, c + 3)
+        s2d(4)
+        s2e(4)
+        s2av(5)
+        s2as(5)
+        s2b(5)
+        s2av(6)
+        s2c(5, "s")
+        s2as(6)
+        s2b(6)
+        s2d(5)
         for g in range(4):
             passes(2, g)
-        s2b(5)
-        s2d(4)
-        s2c(5, "s")
-        s2e(4)
+        s2c(6, "s")
+        s2e(5)
         passes(2, 4)
         passes(2, 5)
-        s2d(5)
-        s2e(5)
-        passes(2, 6)
-        passes(2, 7)
-        s2a(6)
-        s2b(6)
-        for g in range(4):
-            passes(3, g)
-        s2c(6, "s")
         s2d(6)
         s2e(6)
-        for g in range(4, 8):
-            passes(3, g)
+        passes(2, 6)
+        passes(2, 7)
 
         half = NB // 2
         z7a = zt[7 * NB]

@@ -23,9 +23,10 @@ FLOPS = 2 * P * D * R + 2 * P * P * R
 PIN = True
 
 GROUPS = (
-    (0, 2560, 512, (1, 1, 1, 1, 1, 1, 1, 1)),
-    (2560, 1024, 512, (2, 2, 2, 1, 1)),
-    (3584, 512, 256, (4, 2, 1, 1)),
+    (0, 2048, (1, 1, 1, 1, 1, 1, 1, 1)),
+    (2048, 1024, (2, 2, 2, 2)),
+    (3072, 512, (4, 2, 1, 1)),
+    (3584, 512, (4, 2, 1, 1)),
 )
 
 
@@ -39,8 +40,8 @@ def tile_metric_learning_based_adjacency_matrix_w_kernel(
         const = ctx.enter_context(tc.tile_pool(name="const", bufs=1))
         wpool = ctx.enter_context(tc.tile_pool(name="weights", bufs=1))
         work = ctx.enter_context(tc.tile_pool(name="work", bufs=3))
-        zps = ctx.enter_context(tc.psum_pool(name="zps", bufs=6))
-        tps = ctx.enter_context(tc.psum_pool(name="tps", bufs=1))
+        zps = ctx.enter_context(tc.psum_pool(name="zps", bufs=5))
+        tps = ctx.enter_context(tc.psum_pool(name="tps", bufs=2))
         gps = ctx.enter_context(tc.psum_pool(name="gps", bufs=1))
 
         planes = const.tile([P, 2, R], U8, align_bytes=64, name="planes")
@@ -62,13 +63,13 @@ def tile_metric_learning_based_adjacency_matrix_w_kernel(
         for h in range(2):
             nc.sync.dma_start(out=x_sb[h][:], in_=features[:, h * (D // 2) : (h + 1) * (D // 2)])
         for h in range(2):
-            for q in range(1):
+            for q in range(2):
                 nc.sync.dma_start(
                     out=planes[32 * q : 32 * q + 16, h, :].bitcast(I32),
                     in_=P_scales[4 * h : 4 * h + 4, 4 * q : 4 * q + 4, :].bitcast(I32),
                 )
         by_row = P_scales.rearrange("(h s) q n -> q s h n", h=2)
-        for q in range(1, 4):
+        for q in range(2, 4):
             for r in range(4):
                 nc.gpsimd.dma_start(
                     out=planes[32 * q + r : 32 * q + r + 16 : 4, :, :].bitcast(F32),
@@ -76,7 +77,7 @@ def tile_metric_learning_based_adjacency_matrix_w_kernel(
                 )
         words = P_words.rearrange("g p n t -> g p (n t)").bitcast(I32)
         wt = {}
-        for gi, (c0, ncols, width, cuts) in enumerate(GROUPS):
+        for gi, (c0, ncols, cuts) in enumerate(GROUPS):
             g0 = 0
             for ng in cuts:
                 t = wpool.tile([P, ng, ncols], U32, align_bytes=64, name="w%d_%d" % (gi, g0))
@@ -120,7 +121,7 @@ def tile_metric_learning_based_adjacency_matrix_w_kernel(
             fq.append(c_t)
             fs.append(s_t)
 
-        ncol = const.tile([P, 9], F32, name="ncol")
+        ncol = const.tile([P, 8], F32, name="ncol")
         gram = gps.tile([P, P], F32, name="gram")
         zt = {}
         zb = {}
@@ -129,32 +130,32 @@ def tile_metric_learning_based_adjacency_matrix_w_kernel(
         zq = {}
 
         def passes(gi, g):
-            c0, ncols, width, cuts = GROUPS[gi]
+            c0, ncols, cuts = GROUPS[gi]
             t, j = wt[(gi, g)]
             k = 4 * (g % 4)
             h = g // 4
-            for b in range(ncols // width):
-                col = c0 + b * width
+            for b in range(ncols // NB):
+                c = c0 // NB + b
                 if g == 0:
-                    zt[col] = zps.tile([P, NB], F32, tag="z", name="z%d" % col)
+                    zt[c] = zps.tile([P, NB], F32, tag="z", name="z%d" % c)
                 nc.tensor.matmul_mx(
-                    out=zt[col][:, 0:width],
+                    out=zt[c][:],
                     lhsT=fq[g // 2][:, (g % 2) * P : (g % 2 + 1) * P].bitcast(FP8X4),
                     lhsT_scale=fs[g // 2][:, (g % 2) * P : (g % 2 + 1) * P],
-                    rhs=t[:, j, b * width : (b + 1) * width].bitcast(FP8X4),
-                    rhs_scale=planes[k:P, h, col : col + width],
+                    rhs=t[:, j, b * NB : (b + 1) * NB].bitcast(FP8X4),
+                    rhs_scale=planes[k:P, h, c * NB : (c + 1) * NB],
                     start=(g == 0),
                     stop=(g == KG - 1),
                 )
 
         def s2av(c):
             zb[c] = work.tile([P, NB], BF16, tag="zb", bufs=4, name="zb%d" % c)
-            nc.vector.tensor_copy(out=zb[c][:], in_=zt[c * NB][:])
+            nc.vector.tensor_copy(out=zb[c][:], in_=zt[c][:])
 
         def s2as(c):
             junk = work.tile([P, NB], BF16, tag="junk", bufs=2, name="junk%d" % c)
             nc.scalar.activation(
-                out=junk[:], in_=zt[c * NB][:], func=ACT.Square, accum_out=ncol[:, c : c + 1]
+                out=junk[:], in_=zt[c][:], func=ACT.Square, accum_out=ncol[:, c : c + 1]
             )
 
         def s2b(c):
@@ -201,61 +202,67 @@ def tile_metric_learning_based_adjacency_matrix_w_kernel(
         s2as(1)
         passes(1, 0)
         passes(1, 1)
-        for c in range(1, 5):
-            s2b(c)
-            if c < 4:
-                s2av(c + 1)
-            s2d(c - 1)
-            s2c(c, "s")
-            if c < 4:
-                s2as(c + 1)
-            s2e(c - 1)
-            if c < 3:
-                passes(1, 2 * c)
-                passes(1, 2 * c + 1)
-            else:
-                passes(1, c + 3)
-        s2d(4)
-        s2e(4)
+        s2b(1)
+        s2av(2)
+        s2d(0)
+        s2c(1, "s")
+        s2as(2)
+        passes(1, 2)
+        passes(1, 3)
+        s2e(0)
+        s2b(2)
+        s2av(3)
+        s2d(1)
+        s2c(2, "s")
+        s2as(3)
+        passes(1, 4)
+        passes(1, 5)
+        s2e(1)
+        s2b(3)
+        s2d(2)
+        s2c(3, "s")
+        passes(1, 6)
+        passes(1, 7)
+        s2e(2)
+        s2d(3)
+        s2av(4)
+        s2as(4)
+        s2b(4)
         s2av(5)
+        s2c(4, "s")
         s2as(5)
-        s2b(5)
-        s2av(6)
-        s2c(5, "s")
-        s2as(6)
-        s2b(6)
-        s2d(5)
         for g in range(4):
             passes(2, g)
-        s2c(6, "s")
-        s2e(5)
+        s2e(3)
+        s2b(5)
+        s2d(4)
+        s2c(5, "s")
         passes(2, 4)
         passes(2, 5)
-        s2d(6)
-        s2e(6)
+        s2e(4)
+        s2d(5)
         passes(2, 6)
         passes(2, 7)
+        s2av(6)
+        s2as(6)
+        s2b(6)
+        for g in range(4):
+            passes(3, g)
+        s2e(5)
+        s2c(6, "s")
+        s2d(6)
+        for g in range(4, 8):
+            passes(3, g)
+        s2e(6)
 
-        half = NB // 2
-        z7a = zt[7 * NB]
-        z7b = zt[7 * NB + half]
-        zb[7] = work.tile([P, NB], BF16, tag="zb", bufs=4, name="zb7")
-        junk_b = work.tile([P, NB], BF16, tag="junk", bufs=2, name="junk7b")
-        junk_a = work.tile([P, NB], BF16, tag="junk", bufs=2, name="junk7a")
-        nc.vector.tensor_copy(out=zb[7][:, 0:half], in_=z7a[:, 0:half])
-        nc.scalar.activation(
-            out=junk_b[:, 0:half], in_=z7b[:, 0:half], func=ACT.Square, accum_out=ncol[:, 8:9]
-        )
-        nc.vector.tensor_copy(out=zb[7][:, half:NB], in_=z7b[:, 0:half])
-        nc.scalar.activation(
-            out=junk_a[:, 0:half], in_=z7a[:, 0:half], func=ACT.Square, accum_out=ncol[:, 7:8]
-        )
+        s2av(7)
+        s2as(7)
         s2b(7)
+        s2c(7, "v")
         nsum = const.tile([P, 1], F32, name="nsum")
         nc.vector.tensor_reduce(out=nsum[:], in_=ncol[:], axis=AX.X, op=ALU.add)
         njp = zps.tile([P, NB], F32, tag="z", name="njp")
         nc.tensor.transpose(njp[:, 0:P], nsum[:, 0:1].to_broadcast([P, P]), ident[:])
-        s2c(7, "s")
         s2d(7)
         hsum = const.tile([P, P], F32, name="hsum")
         nc.vector.scalar_tensor_tensor(

@@ -30,6 +30,9 @@ GROUPS = (
 )
 
 
+LOAD = 512
+
+
 def tile_metric_learning_based_adjacency_matrix_w_kernel(
     tc, features, P_words, P_scales, out_0, out_1
 ):
@@ -79,14 +82,17 @@ def tile_metric_learning_based_adjacency_matrix_w_kernel(
         wt = {}
         for gi, (c0, ncols, cuts) in enumerate(GROUPS):
             g0 = 0
+            width = min(ncols, LOAD)
             for ng in cuts:
-                t = wpool.tile([P, ng, ncols], U32, align_bytes=64, name="w%d_%d" % (gi, g0))
-                nc.sync.dma_start(
-                    out=t[:].bitcast(I32),
-                    in_=words[g0 : g0 + ng, :, c0 : c0 + ncols].rearrange("g p n -> p g n"),
-                )
-                for j in range(ng):
-                    wt[(gi, g0 + j)] = (t, j)
+                for c1 in range(c0, c0 + ncols, width):
+                    w_t = wpool.tile([P, ng, width], U32, align_bytes=64, name="w%d_%d" % (c1, g0))
+                    nc.sync.dma_start(
+                        out=w_t[:].bitcast(I32),
+                        in_=words[g0 : g0 + ng, :, c1 : c1 + width].rearrange("g p n -> p g n"),
+                    )
+                    for j in range(ng):
+                        for b in range(width // NB):
+                            wt[(c1 // NB + b, g0 + j)] = (w_t, j, b * NB)
                 g0 += ng
 
         fq = []
@@ -131,18 +137,17 @@ def tile_metric_learning_based_adjacency_matrix_w_kernel(
 
         def passes(gi, g):
             c0, ncols, cuts = GROUPS[gi]
-            t, j = wt[(gi, g)]
             k = 4 * (g % 4)
             h = g // 4
-            for b in range(ncols // NB):
-                c = c0 // NB + b
+            for c in range(c0 // NB, (c0 + ncols) // NB):
+                w_t, j, b = wt[(c, g)]
                 if g == 0:
                     zt[c] = zps.tile([P, NB], F32, tag="z", name="z%d" % c)
                 nc.tensor.matmul_mx(
                     out=zt[c][:],
                     lhsT=fq[g // 2][:, (g % 2) * P : (g % 2 + 1) * P].bitcast(FP8X4),
                     lhsT_scale=fs[g // 2][:, (g % 2) * P : (g % 2 + 1) * P],
-                    rhs=t[:, j, b * NB : (b + 1) * NB].bitcast(FP8X4),
+                    rhs=w_t[:, j, b : b + NB].bitcast(FP8X4),
                     rhs_scale=planes[k:P, h, c * NB : (c + 1) * NB],
                     start=(g == 0),
                     stop=(g == KG - 1),

@@ -30,7 +30,8 @@ GROUPS = (
 )
 
 
-LOAD = 512
+HB = 256
+GATE = 3
 
 
 def tile_metric_learning_based_adjacency_matrix_w_kernel(
@@ -80,20 +81,25 @@ def tile_metric_learning_based_adjacency_matrix_w_kernel(
                 )
         words = P_words.rearrange("g p n t -> g p (n t)").bitcast(I32)
         wt = {}
-        for gi, (c0, ncols, cuts) in enumerate(GROUPS):
+        loads = []
+        for c0, ncols, cuts in GROUPS:
             g0 = 0
-            width = min(ncols, LOAD)
             for ng in cuts:
-                for c1 in range(c0, c0 + ncols, width):
-                    w_t = wpool.tile([P, ng, width], U32, align_bytes=64, name="w%d_%d" % (c1, g0))
-                    nc.sync.dma_start(
-                        out=w_t[:].bitcast(I32),
-                        in_=words[g0 : g0 + ng, :, c1 : c1 + width].rearrange("g p n -> p g n"),
-                    )
-                    for j in range(ng):
-                        for b in range(width // NB):
-                            wt[(c1 // NB + b, g0 + j)] = (w_t, j, b * NB)
+                loads.append((c0, ncols, g0, ng))
                 g0 += ng
+        c0, ncols, g0, ng = loads.pop()
+        loads += [(c0, HB, g0, ng), (c0 + HB, HB, g0, ng)]
+        for i, (c0, ncols, g0, ng) in enumerate(loads):
+            w_t = wpool.tile([P, ng, ncols], U32, align_bytes=64, name="w%d_%d" % (c0, g0))
+            if i == GATE:
+                nc.gpsimd.memset(w_t[:, 0, 0:16], 0)
+            nc.sync.dma_start(
+                out=w_t[:].bitcast(I32),
+                in_=words[g0 : g0 + ng, :, c0 : c0 + ncols].rearrange("g p n -> p g n"),
+            )
+            for j in range(ng):
+                for b in range(0, ncols, HB):
+                    wt[((c0 + b) // HB, g0 + j)] = (w_t, j, b)
 
         fq = []
         fs = []
@@ -127,7 +133,7 @@ def tile_metric_learning_based_adjacency_matrix_w_kernel(
             fq.append(c_t)
             fs.append(s_t)
 
-        ncol = const.tile([P, 8], F32, name="ncol")
+        ncol = const.tile([P, 9], F32, name="ncol")
         gram = gps.tile([P, P], F32, name="gram")
         zt = {}
         zb = {}
@@ -139,33 +145,37 @@ def tile_metric_learning_based_adjacency_matrix_w_kernel(
             c0, ncols, cuts = GROUPS[gi]
             k = 4 * (g % 4)
             h = g // 4
-            for c in range(c0 // NB, (c0 + ncols) // NB):
-                w_t, j, b = wt[(c, g)]
+            width = NB if gi < 3 else HB
+            for col in range(c0, c0 + ncols, width):
+                w_t, j, b = wt[(col // HB, g)]
                 if g == 0:
-                    zt[c] = zps.tile([P, NB], F32, tag="z", name="z%d" % c)
+                    zt[col] = zps.tile([P, width], F32, tag="z", name="z%d" % col)
                 nc.tensor.matmul_mx(
-                    out=zt[c][:],
+                    out=zt[col][:],
                     lhsT=fq[g // 2][:, (g % 2) * P : (g % 2 + 1) * P].bitcast(FP8X4),
                     lhsT_scale=fs[g // 2][:, (g % 2) * P : (g % 2 + 1) * P],
-                    rhs=w_t[:, j, b : b + NB].bitcast(FP8X4),
-                    rhs_scale=planes[k:P, h, c * NB : (c + 1) * NB],
+                    rhs=w_t[:, j, b : b + width].bitcast(FP8X4),
+                    rhs_scale=planes[k:P, h, col : col + width],
                     start=(g == 0),
                     stop=(g == KG - 1),
                 )
 
-        def s2av(c):
-            zb[c] = work.tile([P, NB], BF16, tag="zb", bufs=4, name="zb%d" % c)
-            nc.vector.tensor_copy(out=zb[c][:], in_=zt[c][:])
+        def s2av(c, col=0, width=NB):
+            if col == 0:
+                zb[c] = work.tile([P, NB], BF16, tag="zb", bufs=4, name="zb%d" % c)
+            nc.vector.tensor_copy(out=zb[c][:, col : col + width], in_=zt[c * NB + col][:])
 
-        def s2as(c):
-            junk = work.tile([P, NB], BF16, tag="junk", bufs=2, name="junk%d" % c)
+        def s2as(c, col=0, width=NB):
+            junk = work.tile([P, NB], BF16, tag="junk", bufs=2, name="junk%d_%d" % (c, col))
+            i = c + (1 if col else 0)
             nc.scalar.activation(
-                out=junk[:], in_=zt[c][:], func=ACT.Square, accum_out=ncol[:, c : c + 1]
+                out=junk[:, 0:width], in_=zt[c * NB + col][:], func=ACT.Square, accum_out=ncol[:, i : i + 1]
             )
 
-        def s2b(c):
-            tt[c] = tps.tile([P, NB], BF16, tag="t", name="tt%d" % c)
-            for t in range(4):
+        def s2b(c, blocks=range(4)):
+            if 0 in blocks:
+                tt[c] = tps.tile([P, NB], BF16, tag="t", name="tt%d" % c)
+            for t in blocks:
                 nc.tensor.transpose(
                     tt[c][:, t * P : (t + 1) * P], zb[c][:, t * P : (t + 1) * P], identb[:]
                 )
@@ -260,9 +270,12 @@ def tile_metric_learning_based_adjacency_matrix_w_kernel(
             passes(3, g)
         s2e(6)
 
-        s2av(7)
-        s2as(7)
-        s2b(7)
+        s2av(7, 0, HB)
+        s2as(7, 0, HB)
+        s2b(7, range(0, 2))
+        s2av(7, HB, HB)
+        s2as(7, HB, HB)
+        s2b(7, range(2, 4))
         s2c(7, "v")
         nsum = const.tile([P, 1], F32, name="nsum")
         nc.vector.tensor_reduce(out=nsum[:], in_=ncol[:], axis=AX.X, op=ALU.add)

@@ -23,13 +23,10 @@ FLOPS = 2 * P * D * R + 2 * P * P * R
 PIN = True
 
 GROUPS = (
-    (0, 2048, (1, 1, 1, 1, 1, 1, 1, 1)),
-    (2048, 1024, (2, 2, 2, 2)),
-    (3072, 512, (4, 2, 1, 1)),
+    (0, 2560, (1, 1, 1, 1, 1, 1, 1, 1)),
+    (2560, 1024, (2, 2, 2, 2)),
     (3584, 512, (4, 2, 1, 1)),
 )
-
-
 HB = 256
 GATE = 3
 
@@ -141,12 +138,14 @@ def tile_metric_learning_based_adjacency_matrix_w_kernel(
         gz = {}
         zq = {}
 
-        def passes(gi, g):
+        def passes(gi, g, only=None):
             c0, ncols, cuts = GROUPS[gi]
             k = 4 * (g % 4)
             h = g // 4
-            width = NB if gi < 3 else HB
+            width = NB if gi < 2 else HB
             for col in range(c0, c0 + ncols, width):
+                if only is not None and col not in only:
+                    continue
                 w_t, j, b = wt[(col // HB, g)]
                 if g == 0:
                     zt[col] = zps.tile([P, width], F32, tag="z", name="z%d" % col)
@@ -190,8 +189,8 @@ def tile_metric_learning_based_adjacency_matrix_w_kernel(
                 nc.scalar.copy(out=dst, in_=src)
 
         def s2d(c):
-            w_t = work.tile([P, P], U32, tag="zq", align_bytes=64, name="zq%d" % c)
-            s_t = work.tile([P, P], U8, tag="zs", align_bytes=64, name="zs%d" % c)
+            w_t = work.tile([P, P], U32, tag="zq", bufs=4, align_bytes=64, name="zq%d" % c)
+            s_t = work.tile([P, P], U8, tag="zs", bufs=4, align_bytes=64, name="zs%d" % c)
             nc.vector.quantize_mx(out=w_t[:].bitcast(FP8X4), scales=s_t[:], in_=gz[c][:])
             zq[c] = (w_t, s_t)
 
@@ -215,67 +214,62 @@ def tile_metric_learning_based_adjacency_matrix_w_kernel(
         s2av(1)
         s2c(0, "s")
         s2as(1)
-        passes(1, 0)
-        passes(1, 1)
+        passes(1, 0, only=(2560,))
         s2b(1)
         s2av(2)
         s2d(0)
         s2c(1, "s")
         s2as(2)
-        passes(1, 2)
-        passes(1, 3)
-        s2e(0)
+        passes(1, 0, only=(3072,))
+        passes(1, 1)
         s2b(2)
         s2av(3)
         s2d(1)
         s2c(2, "s")
         s2as(3)
-        passes(1, 4)
-        passes(1, 5)
-        s2e(1)
+        s2e(0)
         s2b(3)
+        s2av(4)
         s2d(2)
         s2c(3, "s")
+        s2as(4)
+        passes(1, 2)
+        passes(1, 3)
+        s2e(1)
+        s2b(4)
+        s2d(3)
+        s2c(4, "s")
+        passes(1, 4)
+        passes(1, 5)
+        s2e(2)
+        s2e(3)
+        s2d(4)
         passes(1, 6)
         passes(1, 7)
-        s2e(2)
-        s2d(3)
-        s2av(4)
-        s2as(4)
-        s2b(4)
         s2av(5)
-        s2c(4, "s")
-        s2as(5)
-        for g in range(4):
-            passes(2, g)
-        s2e(3)
-        s2b(5)
-        s2d(4)
-        s2c(5, "s")
-        passes(2, 4)
-        passes(2, 5)
         s2e(4)
-        s2d(5)
-        passes(2, 6)
-        passes(2, 7)
+        s2b(5)
         s2av(6)
-        s2as(6)
+        s2c(5, "s")
+        s2as(5)
+        passes(2, 0)
+        passes(2, 1)
         s2b(6)
-        for g in range(4):
-            passes(3, g)
-        s2e(5)
+        s2d(5)
         s2c(6, "s")
+        s2as(6)
+        for g in range(2, KG):
+            passes(2, g)
         s2d(6)
-        for g in range(4, 8):
-            passes(3, g)
-        s2e(6)
 
         s2av(7, 0, HB)
         s2as(7, 0, HB)
+        s2e(5)
         s2b(7, range(0, 2))
         s2av(7, HB, HB)
         s2as(7, HB, HB)
         s2b(7, range(2, 4))
+        s2e(6)
         s2c(7, "v")
         nsum = const.tile([P, 1], F32, name="nsum")
         nc.vector.tensor_reduce(out=nsum[:], in_=ncol[:], axis=AX.X, op=ALU.add)

@@ -45,7 +45,7 @@ def tile_metric_learning_based_adjacency_matrix_w_kernel(
         tps = ctx.enter_context(tc.psum_pool(name="tps", bufs=2))
         gps = ctx.enter_context(tc.psum_pool(name="gps", bufs=1))
 
-        planes = const.tile([P, 2, R], U8, align_bytes=64, name="planes")
+        planes = const.tile([P, 2, R], U8, align_bytes=256, name="planes")
         nc.vector.memset(planes[:].bitcast(I32), 0)
         one = const.tile([P, 1], F32, name="one")
         nc.vector.memset(one[:], 1.0)
@@ -60,7 +60,7 @@ def tile_metric_learning_based_adjacency_matrix_w_kernel(
         negdiag = const.tile([P, P], F32, name="negdiag")
         nc.vector.tensor_single_scalar(out=negdiag[:], in_=ident[:], scalar=-3.0e38, op=ALU.mult)
 
-        x_sb = [const.tile([P, D // 2], BF16, name="x%d" % h) for h in range(2)]
+        x_sb = [const.tile([P, D // 2], BF16, align_bytes=256, name="x%d" % h) for h in range(2)]
         for h in range(2):
             nc.sync.dma_start(out=x_sb[h][:], in_=features[:, h * (D // 2) : (h + 1) * (D // 2)])
         for h in range(2):
@@ -87,7 +87,7 @@ def tile_metric_learning_based_adjacency_matrix_w_kernel(
         c0, ncols, g0, ng = loads.pop()
         loads += [(c0, HB, g0, ng), (c0 + HB, HB, g0, ng)]
         for i, (c0, ncols, g0, ng) in enumerate(loads):
-            w_t = wpool.tile([P, ng, ncols], U32, align_bytes=64, name="w%d_%d" % (c0, g0))
+            w_t = wpool.tile([P, ng, ncols], U32, align_bytes=256, name="w%d_%d" % (c0, g0))
             if i == GATE:
                 nc.gpsimd.memset(w_t[:, 0, 0:16], 0)
             nc.sync.dma_start(

from contextlib import ExitStack

import concourse.mybir as mybir
from concourse.masks import make_identity

F32 = mybir.dt.float32
BF16 = mybir.dt.bfloat16
I32 = mybir.dt.int32
U32 = mybir.dt.uint32
U8 = mybir.dt.uint8
FP8X4 = mybir.dt.float8_e4m3fn_x4
ACT = mybir.ActivationFunctionType
ALU = mybir.AluOpType
AX = mybir.AxisListType

P = 128
D = 4096
R = 4096
KG = 8
NB = 512
FLOPS = 2 * P * D * R + 2 * P * P * R

PIN = True

GROUPS = (
    (0, 2560, (1, 1, 1, 1, 1, 1, 1, 1)),
    (2560, 1024, (2, 2, 2, 2)),
    (3584, 512, (4, 2, 1, 1)),
)
HB = 256
GATE = 3


def tile_metric_learning_based_adjacency_matrix_w_kernel(
    tc, features, P_words, P_scales, out_0, out_1
):
    nc = tc.nc
    with ExitStack() as ctx:
        if PIN:
            ctx.enter_context(tc.manual_schedule())
        const = ctx.enter_context(tc.tile_pool(name="const", bufs=1))
        wpool = ctx.enter_context(tc.tile_pool(name="weights", bufs=1))
        work = ctx.enter_context(tc.tile_pool(name="work", bufs=3))
        zps = ctx.enter_context(tc.psum_pool(name="zps", bufs=5))
        tps = ctx.enter_context(tc.psum_pool(name="tps", bufs=2))
        gps = ctx.enter_context(tc.psum_pool(name="gps", bufs=1))

        planes = const.tile([P, 2, R], U8, align_bytes=256, name="planes")
        nc.vector.memset(planes[:].bitcast(I32), 0)
        one = const.tile([P, 1], F32, name="one")
        nc.vector.memset(one[:], 1.0)
        mhalf = const.tile([P, 1], F32, name="mhalf")
        nc.vector.memset(mhalf[:], -0.5)
        warm = const.tile([P, 1], F32, name="warm")
        nc.scalar.activation(out=warm[:], in_=one[:], func=ACT.Sqrt)
        ident = const.tile([P, P], F32, name="ident")
        make_identity(nc, ident[:])
        identb = const.tile([P, P], BF16, name="identb")
        nc.vector.tensor_copy(out=identb[:], in_=ident[:])
        negdiag = const.tile([P, P], F32, name="negdiag")
        nc.vector.tensor_single_scalar(out=negdiag[:], in_=ident[:], scalar=-3.0e38, op=ALU.mult)

        x_sb = [const.tile([P, D // 2], BF16, align_bytes=256, name="x%d" % h) for h in range(2)]
        for h in range(2):
            nc.sync.dma_start(out=x_sb[h][:], in_=features[:, h * (D // 2) : (h + 1) * (D // 2)])
        for h in range(2):
            for q in range(2):
                nc.sync.dma_start(
                    out=planes[32 * q : 32 * q + 16, h, :].bitcast(I32),
                    in_=P_scales[4 * h : 4 * h + 4, 4 * q : 4 * q + 4, :].bitcast(I32),
                )
        by_row = P_scales.rearrange("(h s) q n -> q s h n", h=2)
        for q in range(2, 4):
            for r in range(4):
                nc.gpsimd.dma_start(
                    out=planes[32 * q + r : 32 * q + r + 16 : 4, :, :].bitcast(F32),
                    in_=by_row[4 * q + r].bitcast(F32),
                )
        words = P_words.rearrange("g p n t -> g p (n t)").bitcast(I32)
        wt = {}
        loads = []
        for c0, ncols, cuts in GROUPS:
            g0 = 0
            for ng in cuts:
                loads.append((c0, ncols, g0, ng))
                g0 += ng
        c0, ncols, g0, ng = loads.pop()
        loads += [(c0, HB, g0, ng), (c0 + HB, HB, g0, ng)]
        for i, (c0, ncols, g0, ng) in enumerate(loads):
            w_t = wpool.tile([P, ng, ncols], U32, align_bytes=256, name="w%d_%d" % (c0, g0))
            if i == GATE:
                nc.gpsimd.memset(w_t[:, 0, 0:16], 0)
            nc.sync.dma_start(
                out=w_t[:].bitcast(I32),
                in_=words[g0 : g0 + ng, :, c0 : c0 + ncols].rearrange("g p n -> p g n"),
            )
            for j in range(ng):
                for b in range(0, ncols, HB):
                    wt[((c0 + b) // HB, g0 + j)] = (w_t, j, b)

        fq = []
        fs = []
        gf = []
        ft = []
        for j in range(4):
            xw = x_sb[j // 2][:].bitcast(F32)
            tp = zps.tile([P, NB], F32, tag="z", name="ft%d" % j)
            for gl in range(2):
                base = 256 * ((2 * j + gl) % 4)
                for u in range(2):
                    nc.tensor.transpose(
                        tp[:, (2 * gl + u) * P : (2 * gl + u + 1) * P],
                        xw[:, base + u : base + 256 : 2],
                        ident[:],
                    )
            ft.append(tp)
        for j in range(4):
            g_t = const.tile([P, 1024], BF16, align_bytes=64, name="gf%d" % j)
            dst = g_t[:].bitcast(F32).rearrange("p (g i u) -> p g i u", g=2, u=2)
            src = ft[j][:].rearrange("p (g u i) -> p g i u", g=2, u=2)
            if j % 2 == 0:
                nc.vector.tensor_copy(out=dst, in_=src)
            else:
                nc.scalar.copy(out=dst, in_=src)
            gf.append(g_t)
        for j in range(4):
            c_t = const.tile([P, 256], U32, align_bytes=64, name="fq%d" % j)
            s_t = const.tile([P, 256], U8, align_bytes=64, name="fs%d" % j)
            nc.vector.quantize_mx(out=c_t[:].bitcast(FP8X4), scales=s_t[:], in_=gf[j][:])
            fq.append(c_t)
            fs.append(s_t)

        ncol = const.tile([P, 9], F32, name="ncol")
        gram = gps.tile([P, P], F32, name="gram")
        zt = {}
        zb = {}
        tt = {}
        gz = {}
        zq = {}

        def passes(gi, g, only=None):
            c0, ncols, cuts = GROUPS[gi]
            k = 4 * (g % 4)
            h = g // 4
            width = NB if gi < 2 else HB
            for col in range(c0, c0 + ncols, width):
                if only is not None and col not in only:
                    continue
                w_t, j, b = wt[(col // HB, g)]
                if g == 0:
                    zt[col] = zps.tile([P, width], F32, tag="z", name="z%d" % col)
                nc.tensor.matmul_mx(
                    out=zt[col][:],
                    lhsT=fq[g // 2][:, (g % 2) * P : (g % 2 + 1) * P].bitcast(FP8X4),
                    lhsT_scale=fs[g // 2][:, (g % 2) * P : (g % 2 + 1) * P],
                    rhs=w_t[:, j, b : b + width].bitcast(FP8X4),
                    rhs_scale=planes[k:P, h, col : col + width],
                    start=(g == 0),
                    stop=(g == KG - 1),
                )

        def s2av(c, col=0, width=NB):
            if col == 0:
                zb[c] = work.tile([P, NB], BF16, tag="zb", bufs=4, name="zb%d" % c)
            nc.vector.tensor_copy(out=zb[c][:, col : col + width], in_=zt[c * NB + col][:])

        def s2as(c, col=0, width=NB):
            junk = work.tile([P, NB], BF16, tag="junk", bufs=2, name="junk%d_%d" % (c, col))
            i = c + (1 if col else 0)
            nc.scalar.activation(
                out=junk[:, 0:width], in_=zt[c * NB + col][:], func=ACT.Square, accum_out=ncol[:, i : i + 1]
            )

        def s2b(c, blocks=range(4)):
            if 0 in blocks:
                tt[c] = tps.tile([P, NB], BF16, tag="t", name="tt%d" % c)
            for t in blocks:
                nc.tensor.transpose(
                    tt[c][:, t * P : (t + 1) * P], zb[c][:, t * P : (t + 1) * P], identb[:]
                )

        def s2c(c, eng):
            gz[c] = work.tile([P, NB], BF16, tag="gz", align_bytes=64, name="gz%d" % c)
            dst = gz[c][:].rearrange("p (i t) -> p i t", t=4)
            src = tt[c][:].rearrange("p (t i) -> p i t", t=4)
            if eng == "v":
                nc.vector.tensor_copy(out=dst, in_=src)
            else:
                nc.scalar.copy(out=dst, in_=src)

        def s2d(c):
            w_t = work.tile([P, P], U32, tag="zq", bufs=4, align_bytes=64, name="zq%d" % c)
            s_t = work.tile([P, P], U8, tag="zs", bufs=4, align_bytes=64, name="zs%d" % c)
            nc.vector.quantize_mx(out=w_t[:].bitcast(FP8X4), scales=s_t[:], in_=gz[c][:])
            zq[c] = (w_t, s_t)

        def s2e(c):
            w_t, s_t = zq[c]
            nc.tensor.matmul_mx(
                out=gram[:],
                lhsT=w_t[:].bitcast(FP8X4),
                lhsT_scale=s_t[:],
                rhs=w_t[:].bitcast(FP8X4),
                rhs_scale=s_t[:],
                start=(c == 0),
                stop=(c == 7),
            )

        for g in range(KG):
            passes(0, g)
        s2av(0)
        s2as(0)
        s2b(0)
        s2av(1)
        s2c(0, "s")
        s2as(1)
        passes(1, 0, only=(2560,))
        s2b(1)
        s2av(2)
        s2d(0)
        s2c(1, "s")
        s2as(2)
        passes(1, 0, only=(3072,))
        passes(1, 1)
        s2b(2)
        s2av(3)
        s2d(1)
        s2c(2, "s")
        s2as(3)
        s2e(0)
        s2b(3)
        s2av(4)
        s2d(2)
        s2c(3, "s")
        s2as(4)
        passes(1, 2)
        passes(1, 3)
        s2e(1)
        s2b(4)
        s2d(3)
        s2c(4, "s")
        passes(1, 4)
        passes(1, 5)
        s2e(2)
        s2e(3)
        s2d(4)
        passes(1, 6)
        passes(1, 7)
        s2av(5)
        s2e(4)
        s2b(5)
        s2av(6)
        s2c(5, "s")
        s2as(5)
        passes(2, 0)
        passes(2, 1)
        s2b(6)
        s2d(5)
        s2c(6, "s")
        s2as(6)
        for g in range(2, KG):
            passes(2, g)
        s2d(6)

        s2av(7, 0, HB)
        s2as(7, 0, HB)
        s2e(5)
        s2b(7, range(0, 2))
        s2av(7, HB, HB)
        s2as(7, HB, HB)
        s2b(7, range(2, 4))
        s2e(6)
        s2c(7, "v")
        nsum = const.tile([P, 1], F32, name="nsum")
        nc.vector.tensor_reduce(out=nsum[:], in_=ncol[:], axis=AX.X, op=ALU.add)
        njp = zps.tile([P, NB], F32, tag="z", name="njp")
        nc.tensor.transpose(njp[:, 0:P], nsum[:, 0:1].to_broadcast([P, P]), ident[:])
        s2d(7)
        hsum = const.tile([P, P], F32, name="hsum")
        nc.vector.scalar_tensor_tensor(
            out=hsum[:], in0=njp[:, 0:P], scalar=nsum[:, 0:1], in1=negdiag[:], op0=ALU.add, op1=ALU.add
        )
        s2e(7)
        sq = const.tile([P, P], F32, name="sq")
        nc.vector.scalar_tensor_tensor(
            out=sq[:], in0=gram[:], scalar=-2.0, in1=hsum[:], op0=ALU.mult, op1=ALU.add
        )
        sqc = const.tile([P, P], F32, name="sqc")
        nc.vector.tensor_scalar(
            out=sqc[:], in0=sq[:], scalar1=1.0e-30, scalar2=1.0e35, op0=ALU.max, op1=ALU.min
        )
        dist = const.tile([P, P], F32, name="dist")
        nc.scalar.activation(out=dist[:], in_=sqc[:], func=ACT.Sqrt)
        araw = const.tile([P, P], F32, name="araw")
        deg = const.tile([P, 1], F32, name="deg")
        nc.scalar.activation(out=araw[:], in_=dist[:], func=ACT.Exp, scale=-1.0, accum_out=deg[:])
        dinv = const.tile([P, 1], F32, name="dinv")
        nc.gpsimd.tensor_tensor(out=dinv[:], in0=deg[:], in1=mhalf[:], op=ALU.pow)
        adj = const.tile([P, P], F32, name="adj")
        nc.vector.tensor_tensor(out=adj[:], in0=araw[:], in1=ident[:], op=ALU.max)
        nc.sync.dma_start(out=out_1[:, :], in_=adj[:])
        djp = zps.tile([P, NB], F32, tag="z", name="djp")
        nc.tensor.transpose(djp[:, 0:P], dinv[:, 0:1].to_broadcast([P, P]), ident[:])
        norm = const.tile([P, P], F32, name="norm")
        nc.vector.scalar_tensor_tensor(
            out=norm[:], in0=adj[:], scalar=dinv[:, 0:1], in1=djp[:, 0:P], op0=ALU.mult, op1=ALU.mult
        )
        nc.sync.dma_start(out=out_0[:, :], in_=norm[:])
